import numpy as np
import ml_dtypes


def mxq(x, axis, fmt="e4m3"):
    dtype, down = {"e4m3": (ml_dtypes.float8_e4m3fn, 7), "e5m2": (ml_dtypes.float8_e5m2, 14)}[fmt]
    v = np.moveaxis(np.asarray(x, np.float32).astype(ml_dtypes.bfloat16).astype(np.float64), axis, -1)
    blocks = v.reshape(v.shape[:-1] + (-1, 32))
    amax = np.abs(blocks).max(-1, keepdims=True)
    byte = np.maximum(np.where(amax > 0, np.frexp(amax)[1] - 1 + 127, 0) - down, 1)
    scale = np.exp2(byte - 127.0)
    codes = (blocks / scale).astype(np.float32).astype(dtype).astype(np.float64)
    return np.moveaxis((codes * scale).reshape(v.shape), -1, axis)


WIDE = False


def mx_kscale(k):
    if not WIDE:
        return np.ones(k)
    levels = np.array([10, -10, 5, -5, 0])
    a = np.random.permutation(np.resize(levels, k // 512 * 4)).reshape(k // 512, 4)
    idx = np.arange(k)
    return np.exp2(a[idx // 512, idx % 128 // 32])


BF16 = ml_dtypes.bfloat16


def bf(x):
    return np.asarray(x, np.float32).astype(BF16)


def f64(x):
    return np.asarray(x).astype(np.float64)


B, N, D, F, C, L = 2048, 6144, 1024, 256, 128, 28
EPS = 1e-12


def l2norm(x):
    n = np.sqrt(np.sum(x * x, axis=1, keepdims=True))
    return x / np.maximum(n, EPS)


def setup_inputs():
    s = mx_kscale(D)
    return {"features": bf(np.random.standard_normal((B, D)) * s),
            "ex_features": bf(np.random.standard_normal((N, D)) * s),
            "g_weight": bf(np.random.standard_normal((F, D)) / np.sqrt(D) / s)}


def reference(features, ex_features, g_weight):
    gq = mxq(f64(g_weight), 1, "e4m3")
    f = mxq(f64(features), 1, "e4m3") @ gq.T
    exf = mxq(f64(ex_features), 1, "e4m3") @ gq.T
    return l2norm(f), l2norm(exf)

@@ -1,0 +1,201 @@
+import concourse.mybir as mybir
+from concourse.masks import make_identity
+
+F32 = mybir.dt.float32
+BF16 = mybir.dt.bfloat16
+U32 = mybir.dt.uint32
+U8 = mybir.dt.uint8
+FP8X4 = mybir.dt.float8_e4m3fn_x4
+ACT = mybir.ActivationFunctionType
+
+P = 128
+PACK = 4
+K = 1024
+K_PASS = P * PACK
+PASSES = K // K_PASS
+PAIRS = PACK // 2
+BLOCKS = PASSES * PAIRS
+ROW_WORDS = K // 2
+F_OUT = 256
+F_TILES = F_OUT // P
+TILES = 4
+CHUNK_ROWS = P * TILES
+LOADS_AHEAD = 7
+EPS = 1e-12
+
+FLOPS = 2 * (2048 + 6144) * K * F_OUT
+
+
+def transpose_rows(nc, flip_pool, identity, rows_words):
+    flipped = flip_pool.tile([P, BLOCKS, P], F32)
+    for b in range(BLOCKS):
+        nc.tensor.transpose(flipped[:, b, :], rows_words[:, b * P : (b + 1) * P], identity[:])
+    return flipped
+
+
+def regroup(copy, flipped, grouped_words):
+    copy(out=grouped_words, in_=flipped[:].rearrange("p (g u) r -> p g r u", u=PAIRS))
+
+
+def tile_minerva_old_pa_t_kernel(tc, features, ex_features, g_weight, out_0, out_1):
+    nc = tc.nc
+
+    chunks = []
+    for src, dst in ((features, out_0), (ex_features, out_1)):
+        for row in range(0, src.shape[0], CHUNK_ROWS):
+            chunks.append((src[row : row + CHUNK_ROWS, :], dst[row : row + CHUNK_ROWS, :]))
+    n_chunks = len(chunks)
+
+    with tc.manual_schedule(), tc.tile_pool(name="keep", bufs=1) as keep, tc.tile_pool(
+        name="x", bufs=LOADS_AHEAD + 1
+    ) as x_pool, tc.tile_pool(name="operand", bufs=3) as operand_pool, tc.tile_pool(
+        name="small", bufs=4
+    ) as small_pool, tc.tile_pool(name="result", bufs=6) as result_pool, tc.psum_pool(
+        name="flip", bufs=4
+    ) as flip_pool, tc.psum_pool(name="product", bufs=4) as product_pool:
+        x_tiles = {}
+        operands = {}
+        products = {}
+        norms = {}
+
+        def load(c):
+            x_sb = x_pool.tile([P, TILES * K], BF16)
+            nc.sync.dma_start(out=x_sb[:], in_=chunks[c][0].rearrange("(p t) k -> p (t k)", t=TILES))
+            x_tiles[c] = x_sb
+
+        def transpose(c):
+            words = x_tiles[c][:].bitcast(F32)
+            return [
+                transpose_rows(nc, flip_pool, identity, words[:, t * ROW_WORDS : (t + 1) * ROW_WORDS])
+                for t in range(TILES)
+            ]
+
+        w_sb = keep.tile([P, F_TILES * K], BF16)
+        nc.sync.dma_start(
+            out=w_sb[:].rearrange("p (j k) -> p j k", j=F_TILES),
+            in_=g_weight.rearrange("(j p) k -> p j k", p=P),
+        )
+        for c in range(LOADS_AHEAD):
+            load(c)
+
+        identity = keep.tile([P, P], F32)
+        make_identity(nc, identity[:])
+
+        one = keep.tile([P, 1], F32)
+        nc.vector.memset(one[:], 1.0)
+        warm = keep.tile([P, 1], F32)
+        nc.scalar.sqrt(out=warm[:], in_=one[:])
+
+        w_grouped = keep.tile([P, PASSES * F_OUT * PACK], BF16, align_bytes=64)
+        w_codes = keep.tile([P, PASSES * F_OUT], U32, align_bytes=64)
+        w_scales = keep.tile([P, PASSES * F_OUT], U8, align_bytes=64)
+        w_words = w_sb[:].bitcast(F32)
+        w_grouped_words = w_grouped[:].bitcast(F32).rearrange(
+            "p (g j r u) -> p j g r u", g=PASSES, j=F_TILES, u=PAIRS
+        )
+        for j in range(F_TILES):
+            w_flipped = transpose_rows(
+                nc, flip_pool, identity, w_words[:, j * ROW_WORDS : (j + 1) * ROW_WORDS]
+            )
+            regroup(nc.vector.tensor_copy, w_flipped, w_grouped_words[:, j])
+        nc.vector.quantize_mx(out=w_codes[:].bitcast(FP8X4), scales=w_scales[:], in_=w_grouped[:])
+
+        def regroup_chunk(c):
+            grouped = operand_pool.tile([P, TILES * K], BF16, align_bytes=64)
+            codes = operand_pool.tile([P, TILES * PASSES * P], U32, align_bytes=64)
+            scales = operand_pool.tile([P, TILES * PASSES * P], U8, align_bytes=64)
+            operands[c] = (grouped, codes, scales)
+            return grouped[:].bitcast(F32).rearrange(
+                "p (t g r u) -> p t g r u", t=TILES, g=PASSES, u=PAIRS
+            )
+
+        def quantise(c, half):
+            grouped, codes, scales = operands[c]
+            n = TILES * PASSES * P // 2
+            nc.vector.quantize_mx(
+                out=codes[:, half * n : (half + 1) * n].bitcast(FP8X4),
+                scales=scales[:, half * n : (half + 1) * n],
+                in_=grouped[:, half * n * PACK : (half + 1) * n * PACK],
+            )
+
+        def multiply(c):
+            grouped, codes, scales = operands[c]
+            banks = []
+            for h in range(TILES // 2):
+                product = product_pool.tile([P, 2, F_OUT], F32)
+                banks.append(product)
+                for s in range(2):
+                    t = 2 * h + s
+                    for g in range(PASSES):
+                        cols = slice((t * PASSES + g) * P, (t * PASSES + g + 1) * P)
+                        outs = slice(g * F_OUT, (g + 1) * F_OUT)
+                        nc.tensor.matmul_mx(
+                            out=product[:, s, :],
+                            lhsT=codes[:, cols].bitcast(FP8X4),
+                            lhsT_scale=scales[:, cols],
+                            rhs=w_codes[:, outs].bitcast(FP8X4),
+                            rhs_scale=w_scales[:, outs],
+                            start=(g == 0),
+                            stop=(g == PASSES - 1),
+                        )
+            products[c] = banks
+
+        def squares(c):
+            sum_sq = small_pool.tile([P, TILES], F32)
+            for t in range(TILES):
+                unread = small_pool.tile([P, F_OUT], F32)
+                nc.scalar.activation(
+                    out=unread[:],
+                    in_=products[c][t // 2][:, t % 2, :],
+                    func=ACT.Square,
+                    accum_out=sum_sq[:, t : t + 1],
+                )
+            norms[c] = sum_sq
+
+        def clamp(c):
+            floored = small_pool.tile([P, TILES], F32)
+            nc.vector.tensor_scalar_max(out=floored[:], in0=norms[c][:], scalar1=EPS * EPS)
+            norms[c] = floored
+
+        def invert(c):
+            inverse_sq = small_pool.tile([P, TILES], F32)
+            nc.vector.reciprocal(out=inverse_sq[:], in_=norms[c][:])
+            norms[c] = inverse_sq
+
+        def scale_and_store(c):
+            inverse = small_pool.tile([P, TILES], F32)
+            nc.scalar.sqrt(out=inverse[:], in_=norms[c][:])
+            result = result_pool.tile([P, TILES * F_OUT], F32)
+            for t in range(TILES):
+                nc.scalar.activation(
+                    out=result[:, t * F_OUT : (t + 1) * F_OUT],
+                    in_=products[c][t // 2][:, t % 2, :],
+                    func=ACT.Copy,
+                    scale=inverse[:, t : t + 1],
+                )
+            nc.sync.dma_start(out=chunks[c][1].rearrange("(p t) f -> p (t f)", t=TILES), in_=result[:])
+
+        for i in range(n_chunks + 2):
+            if i + LOADS_AHEAD < n_chunks:
+                load(i + LOADS_AHEAD)
+            if i < n_chunks:
+                flipped_tiles = transpose(i)
+            if 1 <= i <= n_chunks:
+                multiply(i - 1)
+            if i >= 2:
+                clamp(i - 2)
+            if i < n_chunks:
+                grouped_words = regroup_chunk(i)
+                regroup(nc.vector.tensor_copy, flipped_tiles[0], grouped_words[:, 0])
+            if i >= 2:
+                invert(i - 2)
+            if i < n_chunks:
+                regroup(nc.vector.tensor_copy, flipped_tiles[1], grouped_words[:, 1])
+                regroup(nc.vector.tensor_copy, flipped_tiles[2], grouped_words[:, 2])
+                regroup(nc.scalar.copy, flipped_tiles[3], grouped_words[:, 3])
+                quantise(i, 0)
+                quantise(i, 1)
+            if 1 <= i <= n_chunks:
+                squares(i - 1)
+            if i >= 2:
+                scale_and_store(i - 2)

@@ -20,6 +20,9 @@ F_OUT = 256
 F_TILES = F_OUT // P
 TILES = 4
 CHUNK_ROWS = P * TILES
+BANK_TILES = 2
+BANKS = TILES // BANK_TILES
+HALF_CODES = TILES * PASSES * P // 2
 LOADS_AHEAD = 7
 EPS = 1e-12
 
@@ -51,32 +54,118 @@ def tile_minerva_old_pa_t_kernel(tc, features, ex_features, g_weight, out_0, out
     ) as x_pool, tc.tile_pool(name="operand", bufs=3) as operand_pool, tc.tile_pool(
         name="small", bufs=4
     ) as small_pool, tc.tile_pool(name="result", bufs=6) as result_pool, tc.psum_pool(
-        name="flip", bufs=4
-    ) as flip_pool, tc.psum_pool(name="product", bufs=4) as product_pool:
+        name="flip", bufs=TILES
+    ) as flip_pool, tc.psum_pool(name="product", bufs=2 * BANKS) as product_pool:
         x_tiles = {}
+        flipped_tiles = {}
         operands = {}
         products = {}
-        norms = {}
+        sums = {}
+        results = {}
 
-        def load(c):
+        def load(c, pieces):
             x_sb = x_pool.tile([P, TILES * K], BF16)
-            nc.sync.dma_start(out=x_sb[:], in_=chunks[c][0].rearrange("(p t) k -> p (t k)", t=TILES))
+            width = TILES * K // pieces
+            rows = chunks[c][0].rearrange("(p t) k -> p (t k)", t=TILES)
+            for piece in range(pieces):
+                cols = slice(piece * width, (piece + 1) * width)
+                nc.sync.dma_start(out=x_sb[:, cols], in_=rows[:, cols])
             x_tiles[c] = x_sb
 
         def transpose(c):
             words = x_tiles[c][:].bitcast(F32)
-            return [
+            flipped_tiles[c] = [
                 transpose_rows(nc, flip_pool, identity, words[:, t * ROW_WORDS : (t + 1) * ROW_WORDS])
                 for t in range(TILES)
             ]
+            grouped = operand_pool.tile([P, TILES * K], BF16, align_bytes=64)
+            codes = operand_pool.tile([P, 2 * HALF_CODES], U32, align_bytes=64)
+            scales = operand_pool.tile([P, 2 * HALF_CODES], U8, align_bytes=64)
+            operands[c] = (grouped, codes, scales)
+
+        def regroup_tile(copy, c, t):
+            grouped_words = operands[c][0][:].bitcast(F32).rearrange(
+                "p (t g r u) -> p t g r u", t=TILES, g=PASSES, u=PAIRS
+            )
+            regroup(copy, flipped_tiles[c][t], grouped_words[:, t])
+
+        def quantise(c, half):
+            grouped, codes, scales = operands[c]
+            cols = slice(half * HALF_CODES, (half + 1) * HALF_CODES)
+            nc.vector.quantize_mx(
+                out=codes[:, cols].bitcast(FP8X4),
+                scales=scales[:, cols],
+                in_=grouped[:, half * HALF_CODES * PACK : (half + 1) * HALF_CODES * PACK],
+            )
+
+        def multiply(c):
+            grouped, codes, scales = operands[c]
+            products[c] = []
+            for h in range(BANKS):
+                product = product_pool.tile([P, BANK_TILES, F_OUT], F32)
+                products[c].append(product)
+                for s in range(BANK_TILES):
+                    for g in range(PASSES):
+                        first = ((h * BANK_TILES + s) * PASSES + g) * P
+                        row_cols = slice(first, first + P)
+                        outs = slice(g * F_OUT, (g + 1) * F_OUT)
+                        nc.tensor.matmul_mx(
+                            out=product[:, s, :],
+                            lhsT=codes[:, row_cols].bitcast(FP8X4),
+                            lhsT_scale=scales[:, row_cols],
+                            rhs=w_codes[:, outs].bitcast(FP8X4),
+                            rhs_scale=w_scales[:, outs],
+                            start=(g == 0),
+                            stop=(g == PASSES - 1),
+                        )
+
+        def square_and_sum(c):
+            sum_sq = small_pool.tile([P, TILES], F32)
+            for t in range(TILES):
+                unread = small_pool.tile([P, F_OUT], F32)
+                nc.scalar.activation(
+                    out=unread[:],
+                    in_=products[c][t // BANK_TILES][:, t % BANK_TILES, :],
+                    func=ACT.Square,
+                    accum_out=sum_sq[:, t : t + 1],
+                )
+            sums[c] = sum_sq
+
+        def floor_sums(c):
+            above = small_pool.tile([P, TILES], F32)
+            nc.scalar.activation(out=above[:], in_=sums[c][:], func=ACT.Relu, bias=-EPS * EPS)
+            sums[c] = above
+
+        def inverse_norms(c):
+            inverse = small_pool.tile([P, TILES], F32)
+            nc.scalar.activation(
+                out=inverse[:], in_=sums[c][:], func=ACT.Abs_reciprocal_sqrt, bias=EPS * EPS
+            )
+            sums[c] = inverse
+            result = result_pool.tile([P, TILES * F_OUT], F32)
+            results[c] = result
+
+        def scale(c, h):
+            tiles = slice(h * BANK_TILES, (h + 1) * BANK_TILES)
+            nc.vector.tensor_mul(
+                out=results[c][:].rearrange("p (t f) -> p t f", t=TILES)[:, tiles, :],
+                in0=products[c][h][:],
+                in1=sums[c][:, tiles].unsqueeze(2).to_broadcast([P, BANK_TILES, F_OUT]),
+            )
+
+        def store(c):
+            nc.sync.dma_start(
+                out=chunks[c][1].rearrange("(p t) f -> p (t f)", t=TILES), in_=results[c][:]
+            )
 
         w_sb = keep.tile([P, F_TILES * K], BF16)
         nc.sync.dma_start(
             out=w_sb[:].rearrange("p (j k) -> p j k", j=F_TILES),
             in_=g_weight.rearrange("(j p) k -> p j k", p=P),
         )
-        for c in range(LOADS_AHEAD):
-            load(c)
+        load(0, TILES)
+        for c in range(1, LOADS_AHEAD):
+            load(c, 1)
 
         identity = keep.tile([P, P], F32)
         make_identity(nc, identity[:])
@@ -84,7 +173,7 @@ def tile_minerva_old_pa_t_kernel(tc, features, ex_features, g_weight, out_0, out
         one = keep.tile([P, 1], F32)
         nc.vector.memset(one[:], 1.0)
         warm = keep.tile([P, 1], F32)
-        nc.scalar.sqrt(out=warm[:], in_=one[:])
+        nc.scalar.activation(out=warm[:], in_=one[:], func=ACT.Abs_reciprocal_sqrt)
 
         w_grouped = keep.tile([P, PASSES * F_OUT * PACK], BF16, align_bytes=64)
         w_codes = keep.tile([P, PASSES * F_OUT], U32, align_bytes=64)
@@ -93,109 +182,42 @@ def tile_minerva_old_pa_t_kernel(tc, features, ex_features, g_weight, out_0, out
         w_grouped_words = w_grouped[:].bitcast(F32).rearrange(
             "p (g j r u) -> p j g r u", g=PASSES, j=F_TILES, u=PAIRS
         )
+        w_copies = (nc.vector.tensor_copy, nc.scalar.copy)
         for j in range(F_TILES):
             w_flipped = transpose_rows(
                 nc, flip_pool, identity, w_words[:, j * ROW_WORDS : (j + 1) * ROW_WORDS]
             )
-            regroup(nc.vector.tensor_copy, w_flipped, w_grouped_words[:, j])
+            regroup(w_copies[j], w_flipped, w_grouped_words[:, j])
         nc.vector.quantize_mx(out=w_codes[:].bitcast(FP8X4), scales=w_scales[:], in_=w_grouped[:])
 
-        def regroup_chunk(c):
-            grouped = operand_pool.tile([P, TILES * K], BF16, align_bytes=64)
-            codes = operand_pool.tile([P, TILES * PASSES * P], U32, align_bytes=64)
-            scales = operand_pool.tile([P, TILES * PASSES * P], U8, align_bytes=64)
-            operands[c] = (grouped, codes, scales)
-            return grouped[:].bitcast(F32).rearrange(
-                "p (t g r u) -> p t g r u", t=TILES, g=PASSES, u=PAIRS
-            )
-
-        def quantise(c, half):
-            grouped, codes, scales = operands[c]
-            n = TILES * PASSES * P // 2
-            nc.vector.quantize_mx(
-                out=codes[:, half * n : (half + 1) * n].bitcast(FP8X4),
-                scales=scales[:, half * n : (half + 1) * n],
-                in_=grouped[:, half * n * PACK : (half + 1) * n * PACK],
-            )
-
-        def multiply(c):
-            grouped, codes, scales = operands[c]
-            banks = []
-            for h in range(TILES // 2):
-                product = product_pool.tile([P, 2, F_OUT], F32)
-                banks.append(product)
-                for s in range(2):
-                    t = 2 * h + s
-                    for g in range(PASSES):
-                        cols = slice((t * PASSES + g) * P, (t * PASSES + g + 1) * P)
-                        outs = slice(g * F_OUT, (g + 1) * F_OUT)
-                        nc.tensor.matmul_mx(
-                            out=product[:, s, :],
-                            lhsT=codes[:, cols].bitcast(FP8X4),
-                            lhsT_scale=scales[:, cols],
-                            rhs=w_codes[:, outs].bitcast(FP8X4),
-                            rhs_scale=w_scales[:, outs],
-                            start=(g == 0),
-                            stop=(g == PASSES - 1),
-                        )
-            products[c] = banks
-
-        def squares(c):
-            sum_sq = small_pool.tile([P, TILES], F32)
-            for t in range(TILES):
-                unread = small_pool.tile([P, F_OUT], F32)
-                nc.scalar.activation(
-                    out=unread[:],
-                    in_=products[c][t // 2][:, t % 2, :],
-                    func=ACT.Square,
-                    accum_out=sum_sq[:, t : t + 1],
-                )
-            norms[c] = sum_sq
-
-        def clamp(c):
-            floored = small_pool.tile([P, TILES], F32)
-            nc.vector.tensor_scalar_max(out=floored[:], in0=norms[c][:], scalar1=EPS * EPS)
-            norms[c] = floored
-
-        def invert(c):
-            inverse_sq = small_pool.tile([P, TILES], F32)
-            nc.vector.reciprocal(out=inverse_sq[:], in_=norms[c][:])
-            norms[c] = inverse_sq
-
-        def scale_and_store(c):
-            inverse = small_pool.tile([P, TILES], F32)
-            nc.scalar.sqrt(out=inverse[:], in_=norms[c][:])
-            result = result_pool.tile([P, TILES * F_OUT], F32)
-            for t in range(TILES):
-                nc.scalar.activation(
-                    out=result[:, t * F_OUT : (t + 1) * F_OUT],
-                    in_=products[c][t // 2][:, t % 2, :],
-                    func=ACT.Copy,
-                    scale=inverse[:, t : t + 1],
-                )
-            nc.sync.dma_start(out=chunks[c][1].rearrange("(p t) f -> p (t f)", t=TILES), in_=result[:])
-
         for i in range(n_chunks + 2):
+            fresh = i < n_chunks
+            multiplied = 1 <= i <= n_chunks
+            summed = i >= 2
             if i + LOADS_AHEAD < n_chunks:
-                load(i + LOADS_AHEAD)
-            if i < n_chunks:
-                flipped_tiles = transpose(i)
-            if 1 <= i <= n_chunks:
+                load(i + LOADS_AHEAD, 1)
+            if fresh:
+                transpose(i)
+            if multiplied:
                 multiply(i - 1)
-            if i >= 2:
-                clamp(i - 2)
-            if i < n_chunks:
-                grouped_words = regroup_chunk(i)
-                regroup(nc.vector.tensor_copy, flipped_tiles[0], grouped_words[:, 0])
-            if i >= 2:
-                invert(i - 2)
-            if i < n_chunks:
-                regroup(nc.vector.tensor_copy, flipped_tiles[1], grouped_words[:, 1])
-                regroup(nc.vector.tensor_copy, flipped_tiles[2], grouped_words[:, 2])
-                regroup(nc.scalar.copy, flipped_tiles[3], grouped_words[:, 3])
+            if fresh:
+                regroup_tile(nc.scalar.copy, i, 0)
+            if summed:
+                floor_sums(i - 2)
+            if fresh:
+                regroup_tile(nc.scalar.copy, i, 1)
+            if summed:
+                inverse_norms(i - 2)
+            if fresh:
+                regroup_tile(nc.scalar.copy, i, 2)
+                regroup_tile(nc.vector.tensor_copy, i, 3)
                 quantise(i, 0)
+            if summed:
+                scale(i - 2, 0)
+            if fresh:
                 quantise(i, 1)
-            if 1 <= i <= n_chunks:
-                squares(i - 1)
-            if i >= 2:
-                scale_and_store(i - 2)
+            if summed:
+                scale(i - 2, 1)
+                store(i - 2)
+            if multiplied:
+                square_and_sum(i - 1)

@@ -7,6 +7,7 @@ U32 = mybir.dt.uint32
 U8 = mybir.dt.uint8
 FP8X4 = mybir.dt.float8_e4m3fn_x4
 ACT = mybir.ActivationFunctionType
+ALU = mybir.AluOpType
 
 P = 128
 PACK = 4
@@ -131,26 +132,22 @@ def tile_minerva_old_pa_t_kernel(tc, features, ex_features, g_weight, out_0, out
                 )
             sums[c] = sum_sq
 
-        def floor_sums(c):
-            above = small_pool.tile([P, TILES], F32)
-            nc.scalar.activation(out=above[:], in_=sums[c][:], func=ACT.Relu, bias=-EPS * EPS)
-            sums[c] = above
-
         def inverse_norms(c):
             inverse = small_pool.tile([P, TILES], F32)
-            nc.scalar.activation(
-                out=inverse[:], in_=sums[c][:], func=ACT.Abs_reciprocal_sqrt, bias=EPS * EPS
-            )
+            nc.scalar.activation(out=inverse[:], in_=sums[c][:], func=ACT.Abs_reciprocal_sqrt)
             sums[c] = inverse
             result = result_pool.tile([P, TILES * F_OUT], F32)
             results[c] = result
 
         def scale(c, h):
             tiles = slice(h * BANK_TILES, (h + 1) * BANK_TILES)
-            nc.vector.tensor_mul(
+            nc.vector.scalar_tensor_tensor(
                 out=results[c][:].rearrange("p (t f) -> p t f", t=TILES)[:, tiles, :],
-                in0=products[c][h][:],
-                in1=sums[c][:, tiles].unsqueeze(2).to_broadcast([P, BANK_TILES, F_OUT]),
+                in0=sums[c][:, tiles].unsqueeze(2).to_broadcast([P, BANK_TILES, F_OUT]),
+                scalar=1.0 / EPS,
+                in1=products[c][h][:],
+                op0=ALU.min,
+                op1=ALU.mult,
             )
 
         def store(c):
@@ -202,9 +199,6 @@ def tile_minerva_old_pa_t_kernel(tc, features, ex_features, g_weight, out_0, out
                 multiply(i - 1)
             if fresh:
                 regroup_tile(nc.scalar.copy, i, 0)
-            if summed:
-                floor_sums(i - 2)
-            if fresh:
                 regroup_tile(nc.scalar.copy, i, 1)
             if summed:
                 inverse_norms(i - 2)

@@ -73,16 +73,20 @@ def tile_minerva_old_pa_t_kernel(tc, features, ex_features, g_weight, out_0, out
                 nc.sync.dma_start(out=x_sb[:, cols], in_=rows[:, cols])
             x_tiles[c] = x_sb
 
-        def transpose(c):
-            words = x_tiles[c][:].bitcast(F32)
-            flipped_tiles[c] = [
-                transpose_rows(nc, flip_pool, identity, words[:, t * ROW_WORDS : (t + 1) * ROW_WORDS])
-                for t in range(TILES)
-            ]
+        def begin(c):
             grouped = operand_pool.tile([P, TILES * K], BF16, align_bytes=64)
             codes = operand_pool.tile([P, 2 * HALF_CODES], U32, align_bytes=64)
             scales = operand_pool.tile([P, 2 * HALF_CODES], U8, align_bytes=64)
             operands[c] = (grouped, codes, scales)
+            flipped_tiles[c] = []
+            products[c] = []
+
+        def transpose(c, h):
+            words = x_tiles[c][:].bitcast(F32)
+            for t in range(h * BANK_TILES, (h + 1) * BANK_TILES):
+                flipped_tiles[c].append(
+                    transpose_rows(nc, flip_pool, identity, words[:, t * ROW_WORDS : (t + 1) * ROW_WORDS])
+                )
 
         def regroup_tile(copy, c, t):
             grouped_words = operands[c][0][:].bitcast(F32).rearrange(
@@ -99,26 +103,24 @@ def tile_minerva_old_pa_t_kernel(tc, features, ex_features, g_weight, out_0, out
                 in_=grouped[:, half * HALF_CODES * PACK : (half + 1) * HALF_CODES * PACK],
             )
 
-        def multiply(c):
+        def multiply(c, h):
             grouped, codes, scales = operands[c]
-            products[c] = []
-            for h in range(BANKS):
-                product = product_pool.tile([P, BANK_TILES, F_OUT], F32)
-                products[c].append(product)
-                for s in range(BANK_TILES):
-                    for g in range(PASSES):
-                        first = ((h * BANK_TILES + s) * PASSES + g) * P
-                        row_cols = slice(first, first + P)
-                        outs = slice(g * F_OUT, (g + 1) * F_OUT)
-                        nc.tensor.matmul_mx(
-                            out=product[:, s, :],
-                            lhsT=codes[:, row_cols].bitcast(FP8X4),
-                            lhsT_scale=scales[:, row_cols],
-                            rhs=w_codes[:, outs].bitcast(FP8X4),
-                            rhs_scale=w_scales[:, outs],
-                            start=(g == 0),
-                            stop=(g == PASSES - 1),
-                        )
+            product = product_pool.tile([P, BANK_TILES, F_OUT], F32)
+            products[c].append(product)
+            for s in range(BANK_TILES):
+                for g in range(PASSES):
+                    first = ((h * BANK_TILES + s) * PASSES + g) * P
+                    row_cols = slice(first, first + P)
+                    outs = slice(g * F_OUT, (g + 1) * F_OUT)
+                    nc.tensor.matmul_mx(
+                        out=product[:, s, :],
+                        lhsT=codes[:, row_cols].bitcast(FP8X4),
+                        lhsT_scale=scales[:, row_cols],
+                        rhs=w_codes[:, outs].bitcast(FP8X4),
+                        rhs_scale=w_scales[:, outs],
+                        start=(g == 0),
+                        stop=(g == PASSES - 1),
+                    )
 
         def square_and_sum(c):
             sum_sq = small_pool.tile([P, TILES], F32)
@@ -194,9 +196,12 @@ def tile_minerva_old_pa_t_kernel(tc, features, ex_features, g_weight, out_0, out
             if i + LOADS_AHEAD < n_chunks:
                 load(i + LOADS_AHEAD, 1)
             if fresh:
-                transpose(i)
-            if multiplied:
-                multiply(i - 1)
+                begin(i)
+            for h in range(BANKS):
+                if fresh:
+                    transpose(i, h)
+                if multiplied:
+                    multiply(i - 1, h)
             if fresh:
                 regroup_tile(nc.scalar.copy, i, 0)
                 regroup_tile(nc.scalar.copy, i, 1)

import concourse.mybir as mybir
from concourse.masks import make_identity

F32 = mybir.dt.float32
BF16 = mybir.dt.bfloat16
U32 = mybir.dt.uint32
U8 = mybir.dt.uint8
FP8X4 = mybir.dt.float8_e4m3fn_x4
ACT = mybir.ActivationFunctionType
ALU = mybir.AluOpType

P = 128
PACK = 4
K = 1024
K_PASS = P * PACK
PASSES = K // K_PASS
PAIRS = PACK // 2
BLOCKS = PASSES * PAIRS
ROW_WORDS = K // 2
F_OUT = 256
F_TILES = F_OUT // P
TILES = 4
CHUNK_ROWS = P * TILES
BANK_TILES = 2
BANKS = TILES // BANK_TILES
HALF_CODES = TILES * PASSES * P // 2
LOADS_AHEAD = 7
EPS = 1e-12

FLOPS = 2 * (2048 + 6144) * K * F_OUT


def transpose_rows(nc, flip_pool, identity, rows_words):
    flipped = flip_pool.tile([P, BLOCKS, P], F32)
    for b in range(BLOCKS):
        nc.tensor.transpose(flipped[:, b, :], rows_words[:, b * P : (b + 1) * P], identity[:])
    return flipped


def regroup(copy, flipped, grouped_words):
    copy(out=grouped_words, in_=flipped[:].rearrange("p (g u) r -> p g r u", u=PAIRS))


def tile_minerva_old_pa_t_kernel(tc, features, ex_features, g_weight, out_0, out_1):
    nc = tc.nc

    chunks = []
    for src, dst in ((features, out_0), (ex_features, out_1)):
        for row in range(0, src.shape[0], CHUNK_ROWS):
            chunks.append((src[row : row + CHUNK_ROWS, :], dst[row : row + CHUNK_ROWS, :]))
    n_chunks = len(chunks)

    with tc.manual_schedule(), tc.tile_pool(name="keep", bufs=1) as keep, tc.tile_pool(
        name="x", bufs=LOADS_AHEAD + 1
    ) as x_pool, tc.tile_pool(name="operand", bufs=3) as operand_pool, tc.tile_pool(
        name="small", bufs=4
    ) as small_pool, tc.tile_pool(name="result", bufs=6) as result_pool, tc.psum_pool(
        name="flip", bufs=TILES
    ) as flip_pool, tc.psum_pool(name="product", bufs=2 * BANKS) as product_pool:
        x_tiles = {}
        flipped_tiles = {}
        operands = {}
        products = {}
        sums = {}
        results = {}

        def load(c, pieces):
            x_sb = x_pool.tile([P, TILES * K], BF16)
            width = TILES * K // pieces
            rows = chunks[c][0].rearrange("(p t) k -> p (t k)", t=TILES)
            for piece in range(pieces):
                cols = slice(piece * width, (piece + 1) * width)
                nc.sync.dma_start(out=x_sb[:, cols], in_=rows[:, cols])
            x_tiles[c] = x_sb

        def begin(c):
            grouped = operand_pool.tile([P, TILES * K], BF16, align_bytes=64)
            codes = operand_pool.tile([P, 2 * HALF_CODES], U32, align_bytes=64)
            scales = operand_pool.tile([P, 2 * HALF_CODES], U8, align_bytes=64)
            operands[c] = (grouped, codes, scales)
            flipped_tiles[c] = []
            products[c] = []

        def transpose(c, h):
            words = x_tiles[c][:].bitcast(F32)
            for t in range(h * BANK_TILES, (h + 1) * BANK_TILES):
                flipped_tiles[c].append(
                    transpose_rows(nc, flip_pool, identity, words[:, t * ROW_WORDS : (t + 1) * ROW_WORDS])
                )

        def regroup_tile(copy, c, t):
            grouped_words = operands[c][0][:].bitcast(F32).rearrange(
                "p (t g r u) -> p t g r u", t=TILES, g=PASSES, u=PAIRS
            )
            regroup(copy, flipped_tiles[c][t], grouped_words[:, t])

        def quantise(c, half):
            grouped, codes, scales = operands[c]
            cols = slice(half * HALF_CODES, (half + 1) * HALF_CODES)
            nc.vector.quantize_mx(
                out=codes[:, cols].bitcast(FP8X4),
                scales=scales[:, cols],
                in_=grouped[:, half * HALF_CODES * PACK : (half + 1) * HALF_CODES * PACK],
            )

        def multiply(c, h):
            grouped, codes, scales = operands[c]
            product = product_pool.tile([P, BANK_TILES, F_OUT], F32)
            products[c].append(product)
            for s in range(BANK_TILES):
                for g in range(PASSES):
                    first = ((h * BANK_TILES + s) * PASSES + g) * P
                    row_cols = slice(first, first + P)
                    outs = slice(g * F_OUT, (g + 1) * F_OUT)
                    nc.tensor.matmul_mx(
                        out=product[:, s, :],
                        lhsT=codes[:, row_cols].bitcast(FP8X4),
                        lhsT_scale=scales[:, row_cols],
                        rhs=w_codes[:, outs].bitcast(FP8X4),
                        rhs_scale=w_scales[:, outs],
                        start=(g == 0),
                        stop=(g == PASSES - 1),
                    )

        def square_and_sum(c):
            sum_sq = small_pool.tile([P, TILES], F32)
            for t in range(TILES):
                unread = small_pool.tile([P, F_OUT], F32)
                nc.scalar.activation(
                    out=unread[:],
                    in_=products[c][t // BANK_TILES][:, t % BANK_TILES, :],
                    func=ACT.Square,
                    accum_out=sum_sq[:, t : t + 1],
                )
            sums[c] = sum_sq

        def inverse_norms(c):
            inverse = small_pool.tile([P, TILES], F32)
            nc.scalar.activation(out=inverse[:], in_=sums[c][:], func=ACT.Abs_reciprocal_sqrt)
            sums[c] = inverse
            result = result_pool.tile([P, TILES * F_OUT], F32)
            results[c] = result

        def scale(c, h):
            tiles = slice(h * BANK_TILES, (h + 1) * BANK_TILES)
            nc.vector.scalar_tensor_tensor(
                out=results[c][:].rearrange("p (t f) -> p t f", t=TILES)[:, tiles, :],
                in0=sums[c][:, tiles].unsqueeze(2).to_broadcast([P, BANK_TILES, F_OUT]),
                scalar=1.0 / EPS,
                in1=products[c][h][:],
                op0=ALU.min,
                op1=ALU.mult,
            )

        def store(c):
            nc.sync.dma_start(
                out=chunks[c][1].rearrange("(p t) f -> p (t f)", t=TILES), in_=results[c][:]
            )

        w_sb = keep.tile([P, F_TILES * K], BF16)
        nc.sync.dma_start(
            out=w_sb[:].rearrange("p (j k) -> p j k", j=F_TILES),
            in_=g_weight.rearrange("(j p) k -> p j k", p=P),
        )
        load(0, TILES)
        for c in range(1, LOADS_AHEAD):
            load(c, 1)

        identity = keep.tile([P, P], F32)
        make_identity(nc, identity[:])

        one = keep.tile([P, 1], F32)
        nc.vector.memset(one[:], 1.0)
        warm = keep.tile([P, 1], F32)
        nc.scalar.activation(out=warm[:], in_=one[:], func=ACT.Abs_reciprocal_sqrt)

        w_grouped = keep.tile([P, PASSES * F_OUT * PACK], BF16, align_bytes=64)
        w_codes = keep.tile([P, PASSES * F_OUT], U32, align_bytes=64)
        w_scales = keep.tile([P, PASSES * F_OUT], U8, align_bytes=64)
        w_words = w_sb[:].bitcast(F32)
        w_grouped_words = w_grouped[:].bitcast(F32).rearrange(
            "p (g j r u) -> p j g r u", g=PASSES, j=F_TILES, u=PAIRS
        )
        w_copies = (nc.vector.tensor_copy, nc.scalar.copy)
        for j in range(F_TILES):
            w_flipped = transpose_rows(
                nc, flip_pool, identity, w_words[:, j * ROW_WORDS : (j + 1) * ROW_WORDS]
            )
            regroup(w_copies[j], w_flipped, w_grouped_words[:, j])
        nc.vector.quantize_mx(out=w_codes[:].bitcast(FP8X4), scales=w_scales[:], in_=w_grouped[:])

        for i in range(n_chunks + 2):
            fresh = i < n_chunks
            multiplied = 1 <= i <= n_chunks
            summed = i >= 2
            if i + LOADS_AHEAD < n_chunks:
                load(i + LOADS_AHEAD, 1)
            if fresh:
                begin(i)
            for h in range(BANKS):
                if fresh:
                    transpose(i, h)
                if multiplied:
                    multiply(i - 1, h)
            if fresh:
                regroup_tile(nc.scalar.copy, i, 0)
                regroup_tile(nc.scalar.copy, i, 1)
            if summed:
                inverse_norms(i - 2)
            if fresh:
                regroup_tile(nc.scalar.copy, i, 2)
                regroup_tile(nc.vector.tensor_copy, i, 3)
                quantise(i, 0)
            if summed:
                scale(i - 2, 0)
            if fresh:
                quantise(i, 1)
            if summed:
                scale(i - 2, 1)
                store(i - 2)
            if multiplied:
                square_and_sum(i - 1)
